import numpy as np
import ml_dtypes


def mxq(x, axis, fmt="e4m3"):
    dtype, down = {"e4m3": (ml_dtypes.float8_e4m3fn, 7), "e5m2": (ml_dtypes.float8_e5m2, 14)}[fmt]
    v = np.moveaxis(np.asarray(x, np.float32).astype(ml_dtypes.bfloat16).astype(np.float64), axis, -1)
    blocks = v.reshape(v.shape[:-1] + (-1, 32))
    amax = np.abs(blocks).max(-1, keepdims=True)
    byte = np.maximum(np.where(amax > 0, np.frexp(amax)[1] - 1 + 127, 0) - down, 1)
    scale = np.exp2(byte - 127.0)
    codes = (blocks / scale).astype(np.float32).astype(dtype).astype(np.float64)
    return np.moveaxis((codes * scale).reshape(v.shape), -1, axis)


WIDE = False


def mx_kscale(k):
    if not WIDE:
        return np.ones(k)
    levels = np.array([10, -10, 5, -5, 0])
    a = np.random.permutation(np.resize(levels, k // 512 * 4)).reshape(k // 512, 4)
    idx = np.arange(k)
    return np.exp2(a[idx // 512, idx % 128 // 32])


BF16 = ml_dtypes.bfloat16


def bf(x):
    return np.asarray(x, np.float32).astype(BF16)


def f64(x):
    return np.asarray(x).astype(np.float64)


BS, BLOCK, HID, GAP, G = 4096, 512, 512, 64, 2


def elu(v):
    return np.where(v > 0.0, v, np.exp(np.minimum(v, 0.0)) - 1.0)


def setup_inputs():
    s = mx_kscale(BLOCK)
    s = s / s.max()
    return {"y_lanes": bf((np.random.standard_normal((BS, BLOCK, G)) * 1.3 * s[None, :, None]).reshape(BS, BLOCK * G)),
            "w1": bf(np.random.standard_normal((G, BLOCK, HID)) / np.sqrt(BLOCK) / s[None, :, None]),
            "b1": bf(np.random.standard_normal((G, 1, HID)) * 0.2),
            "w2": bf(np.random.standard_normal((G, HID, BLOCK)) / np.sqrt(HID)),
            "b2": bf(np.random.standard_normal((G, 1, BLOCK)) * 0.2)}


def reference(y_lanes, w1, b1, w2, b2):
    y = f64(y_lanes)
    bs = y.shape[0]
    y = y.reshape(-1, BLOCK, G).transpose(0, 2, 1).reshape(bs, -1)
    z = y.reshape(bs, -1, BLOCK).transpose(1, 0, 2)
    h = elu((mxq(z, 2, "e4m3") @ mxq(f64(w1), 1, "e4m3")) + f64(b1))
    h = (mxq(h, 2, "e4m3") @ mxq(f64(w2), 1, "e4m3")) + f64(b2)
    z = h + z
    y = z.transpose(1, 0, 2).reshape(bs, -1)
    return y.reshape(-1, G, BLOCK).transpose(0, 2, 1).reshape(bs, -1)

@@ -1,0 +1,211 @@
+from contextlib import ExitStack
+
+import concourse.mybir as mybir
+from concourse.masks import make_identity
+
+F32 = mybir.dt.float32
+BF16 = mybir.dt.bfloat16
+U32 = mybir.dt.uint32
+U8 = mybir.dt.uint8
+FP8X4 = mybir.dt.float8_e4m3fn_x4
+ALU = mybir.AluOpType
+ACT = mybir.ActivationFunctionType
+
+P = 128
+PACK = 4
+LANES = 2
+ROWS = 4096
+FEAT = P * PACK
+WIDTH = LANES * FEAT
+CHUNK = 512
+ROW_TILES = CHUNK // P
+N_CHUNKS = ROWS // CHUNK
+HALF = FEAT // 2
+
+FLOPS = 2 * 2 * LANES * ROWS * FEAT * FEAT
+
+
+def quantise_weights(nc, stage, w, codes, scales):
+    raw = stage.tile([P, LANES, PACK, FEAT], BF16, name="raw")
+    nc.sync.dma_start(out=raw[:], in_=w.rearrange("g (t p) n -> p g t n", p=P))
+    for g in range(LANES):
+        grouped = stage.tile([P, FEAT, PACK], BF16, name="grouped", align_bytes=64)
+        nc.vector.tensor_copy(
+            out=grouped.rearrange("p (c i) t -> p c t i", i=4),
+            in_=raw[:, g].rearrange("p t (c i) -> p c t i", i=4),
+        )
+        nc.vector.quantize_mx(
+            out=codes[:, g, :].bitcast(FP8X4),
+            scales=scales[:, g, :],
+            in_=grouped.rearrange("p n t -> p (n t)"),
+        )
+
+
+def tile_blockresmlp_mixerblock_pa_t_kernel(tc, y_lanes, w1, b1, w2, b2, out):
+    nc = tc.nc
+    with ExitStack() as ctx:
+        consts = ctx.enter_context(tc.tile_pool(name="consts", bufs=1))
+        stage = ctx.enter_context(tc.tile_pool(name="stage", bufs=2))
+        y_pool = ctx.enter_context(tc.tile_pool(name="y_pool", bufs=4))
+        res_pool = ctx.enter_context(tc.tile_pool(name="res_pool", bufs=3))
+        z_pool = ctx.enter_context(tc.tile_pool(name="z_pool", bufs=2))
+        elu_pool = ctx.enter_context(tc.tile_pool(name="elu_pool", bufs=2))
+        h_pool = ctx.enter_context(tc.tile_pool(name="h_pool", bufs=2))
+        zt_psum = ctx.enter_context(tc.psum_pool(name="zt_psum", bufs=2))
+        l1_psum = ctx.enter_context(tc.psum_pool(name="l1_psum", bufs=4))
+        l2_psum = ctx.enter_context(tc.psum_pool(name="l2_psum", bufs=2))
+
+        y_tiles = {}
+        res_tiles = {}
+        z_codes = {}
+        h_codes = {}
+
+        def load_rows(c):
+            y_sb = y_pool.tile([P, ROW_TILES, WIDTH], BF16, name="y_sb")
+            nc.sync.dma_start(
+                out=y_sb[:],
+                in_=y_lanes[c * CHUNK : (c + 1) * CHUNK, :].rearrange("(p j) w -> p j w", j=ROW_TILES),
+            )
+            y_tiles[c] = y_sb
+
+        load_rows(0)
+
+        identity = consts.tile([P, P], F32, name="identity")
+        make_identity(nc, identity[:])
+
+        w1_codes = consts.tile([P, LANES, FEAT], U32, name="w1_codes", align_bytes=64)
+        w1_scales = consts.tile([P, LANES, FEAT], U8, name="w1_scales", align_bytes=64)
+        w2_codes = consts.tile([P, LANES, FEAT], U32, name="w2_codes", align_bytes=64)
+        w2_scales = consts.tile([P, LANES, FEAT], U8, name="w2_scales", align_bytes=64)
+        quantise_weights(nc, stage, w1, w1_codes, w1_scales)
+        load_rows(1)
+        quantise_weights(nc, stage, w2, w2_codes, w2_scales)
+
+        b1_rows = consts.tile([P, P], BF16, name="b1_rows")
+        nc.vector.memset(b1_rows[:], 0.0)
+        nc.scalar.dma_start(
+            out=b1_rows[0 : LANES * PACK, :], in_=b1.rearrange("g o (t p) -> (g o t) p", p=P)
+        )
+        b1_rows_f32 = consts.tile([P, P], F32, name="b1_rows_f32")
+        nc.vector.tensor_copy(out=b1_rows_f32[:], in_=b1_rows[:])
+        b1_ps = zt_psum.tile([P, P], F32, name="b1_ps", tag="zt")
+        nc.tensor.transpose(b1_ps[:], b1_rows_f32[:], identity[:])
+        b1_col = consts.tile([P, LANES * PACK], F32, name="b1_col")
+        nc.vector.tensor_copy(out=b1_col[:], in_=b1_ps[:, 0 : LANES * PACK])
+
+        b2_rows = consts.tile([P, LANES, FEAT], BF16, name="b2_rows")
+        nc.scalar.dma_start(
+            out=b2_rows.rearrange("p g d -> p (g d)"),
+            in_=b2.rearrange("g o d -> (g o d)").partition_broadcast(P),
+        )
+        b2_all = consts.tile([P, FEAT, LANES], F32, name="b2_all")
+        nc.vector.tensor_copy(out=b2_all[:], in_=b2_rows.rearrange("p g d -> p d g"))
+
+        def quantise_rows(c):
+            y_sb = y_tiles[c]
+            zg = z_pool.tile([P, LANES, CHUNK, PACK], BF16, name="zg", align_bytes=64)
+            for j in range(ROW_TILES):
+                words = y_sb[:, j, :].bitcast(F32)
+                zt = zt_psum.tile([P, PACK, P], F32, name="zt", tag="zt")
+                for t in range(PACK):
+                    nc.tensor.transpose(zt[:, t, :], words[:, t * P : (t + 1) * P], identity[:])
+                nc.scalar.copy(
+                    out=zg[:, :, j * P : (j + 1) * P, :],
+                    in_=zt[:].bitcast(BF16).rearrange("p t (b g) -> p g b t", g=LANES),
+                )
+            zc = z_pool.tile([P, LANES, CHUNK], U32, name="zc", align_bytes=64)
+            zs = z_pool.tile([P, LANES, CHUNK], U8, name="zs", align_bytes=64)
+            nc.vector.quantize_mx(
+                out=zc.rearrange("p g b -> p (g b)").bitcast(FP8X4),
+                scales=zs.rearrange("p g b -> p (g b)"),
+                in_=zg.rearrange("p g b t -> p (g b t)"),
+            )
+            z_codes[c] = (zc, zs)
+
+        def add_bias_to_rows(c):
+            y_sb = y_tiles[c]
+            res = res_pool.tile([P, ROW_TILES, WIDTH], F32, name="res")
+            for j in range(ROW_TILES):
+                engine = nc.gpsimd if j % 2 == 0 else nc.vector
+                engine.tensor_tensor(
+                    out=res[:, j, :],
+                    in0=y_sb[:, j, :],
+                    in1=b2_all.rearrange("p d g -> p (d g)"),
+                    op=ALU.add,
+                )
+            res_tiles[c] = res
+
+        def hidden_layer(c):
+            zc, zs = z_codes[c]
+            hc = h_pool.tile([P, LANES, CHUNK], U32, name="hc", align_bytes=64)
+            hs = h_pool.tile([P, LANES, CHUNK], U8, name="hs", align_bytes=64)
+            for g in range(LANES):
+                exp_v = elu_pool.tile([P, PACK, CHUNK], F32, name="exp_v")
+                relu_v = elu_pool.tile([P, PACK, CHUNK], F32, name="relu_v")
+                for t in range(PACK):
+                    acc = l1_psum.tile([P, CHUNK], F32, name="acc")
+                    nc.tensor.matmul_mx(
+                        out=acc[:],
+                        lhsT=w1_codes[:, g, t * P : (t + 1) * P].bitcast(FP8X4),
+                        lhsT_scale=w1_scales[:, g, t * P : (t + 1) * P],
+                        rhs=zc[:, g, :].bitcast(FP8X4),
+                        rhs_scale=zs[:, g, :],
+                        start=True,
+                        stop=True,
+                    )
+                    bias = b1_col[:, g * PACK + t : g * PACK + t + 1]
+                    nc.scalar.activation(out=exp_v[:, t, :], in_=acc[:], func=ACT.Exp, bias=bias, scale=1.0)
+                    nc.scalar.activation(out=relu_v[:, t, :], in_=acc[:], func=ACT.Relu, bias=bias, scale=1.0)
+                hg = h_pool.tile([P, CHUNK, PACK], BF16, name="hg", align_bytes=64)
+                nc.vector.scalar_tensor_tensor(
+                    out=hg[:],
+                    in0=exp_v.rearrange("p t b -> p b t"),
+                    scalar=-1.0,
+                    in1=relu_v.rearrange("p t b -> p b t"),
+                    op0=ALU.add,
+                    op1=ALU.min,
+                )
+                nc.vector.quantize_mx(
+                    out=hc[:, g, :].bitcast(FP8X4),
+                    scales=hs[:, g, :],
+                    in_=hg.rearrange("p b t -> p (b t)"),
+                )
+            h_codes[c] = (hc, hs)
+
+        def output_layer(c):
+            hc, hs = h_codes[c]
+            res = res_tiles[c]
+            for j in range(ROW_TILES):
+                for half in range(FEAT // HALF):
+                    prod = l2_psum.tile([P, LANES, HALF], F32, name="prod")
+                    for g in range(LANES):
+                        nc.tensor.matmul_mx(
+                            out=prod[:, g, :],
+                            lhsT=hc[:, g, j * P : (j + 1) * P].bitcast(FP8X4),
+                            lhsT_scale=hs[:, g, j * P : (j + 1) * P],
+                            rhs=w2_codes[:, g, half * HALF : (half + 1) * HALF].bitcast(FP8X4),
+                            rhs_scale=w2_scales[:, g, half * HALF : (half + 1) * HALF],
+                            start=True,
+                            stop=True,
+                        )
+                    cols = res[:, j, half * LANES * HALF : (half + 1) * LANES * HALF].rearrange(
+                        "p (d g) -> p d g", g=LANES
+                    )
+                    nc.vector.tensor_tensor(
+                        out=cols, in0=prod.rearrange("p g d -> p d g"), in1=cols, op=ALU.add
+                    )
+            nc.sync.dma_start(
+                out=out[c * CHUNK : (c + 1) * CHUNK, :].rearrange("(p j) w -> p j w", j=ROW_TILES),
+                in_=res[:],
+            )
+
+        for step in range(N_CHUNKS + 2):
+            if step + 2 < N_CHUNKS:
+                load_rows(step + 2)
+            if step < N_CHUNKS:
+                quantise_rows(step)
+            if 0 <= step - 1 < N_CHUNKS:
+                hidden_layer(step - 1)
+                add_bias_to_rows(step - 1)
+            if 0 <= step - 2 < N_CHUNKS:
+                output_layer(step - 2)

@@ -156,14 +156,14 @@ def tile_blockresmlp_mixerblock_pa_t_kernel(tc, y_lanes, w1, b1, w2, b2, out):
                     bias = b1_col[:, g * PACK + t : g * PACK + t + 1]
                     nc.scalar.activation(out=exp_v[:, t, :], in_=acc[:], func=ACT.Exp, bias=bias, scale=1.0)
                     nc.scalar.activation(out=relu_v[:, t, :], in_=acc[:], func=ACT.Relu, bias=bias, scale=1.0)
-                hg = h_pool.tile([P, CHUNK, PACK], BF16, name="hg", align_bytes=64)
+                h_planes = h_pool.tile([P, PACK, CHUNK], BF16, name="h_planes")
                 nc.vector.scalar_tensor_tensor(
-                    out=hg[:],
-                    in0=exp_v.rearrange("p t b -> p b t"),
-                    scalar=-1.0,
-                    in1=relu_v.rearrange("p t b -> p b t"),
-                    op0=ALU.add,
-                    op1=ALU.min,
+                    out=h_planes[:], in0=exp_v[:], scalar=-1.0, in1=relu_v[:], op0=ALU.add, op1=ALU.min
+                )
+                hg = h_pool.tile([P, CHUNK, PACK], BF16, name="hg", align_bytes=64)
+                nc.vector.tensor_copy(
+                    out=hg.rearrange("p (c i) t -> p c t i", i=4),
+                    in_=h_planes.rearrange("p t (c i) -> p c t i", i=4),
                 )
                 nc.vector.quantize_mx(
                     out=hc[:, g, :].bitcast(FP8X4),

@@ -126,8 +126,7 @@ def tile_blockresmlp_mixerblock_pa_t_kernel(tc, y_lanes, w1, b1, w2, b2, out):
             y_sb = y_tiles[c]
             res = res_pool.tile([P, ROW_TILES, WIDTH], F32, name="res")
             for j in range(ROW_TILES):
-                engine = nc.gpsimd if j % 2 == 0 else nc.vector
-                engine.tensor_tensor(
+                nc.vector.tensor_tensor(
                     out=res[:, j, :],
                     in0=y_sb[:, j, :],
                     in1=b2_all.rearrange("p d g -> p (d g)"),
@@ -156,14 +155,14 @@ def tile_blockresmlp_mixerblock_pa_t_kernel(tc, y_lanes, w1, b1, w2, b2, out):
                     bias = b1_col[:, g * PACK + t : g * PACK + t + 1]
                     nc.scalar.activation(out=exp_v[:, t, :], in_=acc[:], func=ACT.Exp, bias=bias, scale=1.0)
                     nc.scalar.activation(out=relu_v[:, t, :], in_=acc[:], func=ACT.Relu, bias=bias, scale=1.0)
-                h_planes = h_pool.tile([P, PACK, CHUNK], BF16, name="h_planes")
-                nc.vector.scalar_tensor_tensor(
-                    out=h_planes[:], in0=exp_v[:], scalar=-1.0, in1=relu_v[:], op0=ALU.add, op1=ALU.min
-                )
                 hg = h_pool.tile([P, CHUNK, PACK], BF16, name="hg", align_bytes=64)
-                nc.vector.tensor_copy(
-                    out=hg.rearrange("p (c i) t -> p c t i", i=4),
-                    in_=h_planes.rearrange("p t (c i) -> p c t i", i=4),
+                nc.vector.scalar_tensor_tensor(
+                    out=hg[:],
+                    in0=exp_v.rearrange("p t b -> p b t"),
+                    scalar=-1.0,
+                    in1=relu_v.rearrange("p t b -> p b t"),
+                    op0=ALU.add,
+                    op1=ALU.min,
                 )
                 nc.vector.quantize_mx(
                     out=hc[:, g, :].bitcast(FP8X4),

@@ -20,7 +20,8 @@ WIDTH = LANES * FEAT
 CHUNK = 512
 ROW_TILES = CHUNK // P
 N_CHUNKS = ROWS // CHUNK
-HALF = FEAT // 2
+HALVES = 2
+BLOCKS = PACK // HALVES
 
 FLOPS = 2 * 2 * LANES * ROWS * FEAT * FEAT
 
@@ -46,32 +47,47 @@ def tile_blockresmlp_mixerblock_pa_t_kernel(tc, y_lanes, w1, b1, w2, b2, out):
     with ExitStack() as ctx:
         consts = ctx.enter_context(tc.tile_pool(name="consts", bufs=1))
         stage = ctx.enter_context(tc.tile_pool(name="stage", bufs=2))
-        y_pool = ctx.enter_context(tc.tile_pool(name="y_pool", bufs=4))
-        res_pool = ctx.enter_context(tc.tile_pool(name="res_pool", bufs=3))
+        y_pool = ctx.enter_context(tc.tile_pool(name="y_pool", bufs=6))
         z_pool = ctx.enter_context(tc.tile_pool(name="z_pool", bufs=2))
         elu_pool = ctx.enter_context(tc.tile_pool(name="elu_pool", bufs=2))
         h_pool = ctx.enter_context(tc.tile_pool(name="h_pool", bufs=2))
+        rt_pool = ctx.enter_context(tc.tile_pool(name="rt_pool", bufs=3))
+        res_pool = ctx.enter_context(tc.tile_pool(name="res_pool", bufs=2))
         zt_psum = ctx.enter_context(tc.psum_pool(name="zt_psum", bufs=2))
-        l1_psum = ctx.enter_context(tc.psum_pool(name="l1_psum", bufs=4))
+        l1_psum = ctx.enter_context(tc.psum_pool(name="l1_psum", bufs=2))
         l2_psum = ctx.enter_context(tc.psum_pool(name="l2_psum", bufs=2))
+        ot_psum = ctx.enter_context(tc.psum_pool(name="ot_psum", bufs=2))
 
         y_tiles = {}
-        res_tiles = {}
         z_codes = {}
         h_codes = {}
 
+        def chunk_rows(dram, c):
+            return dram[c * CHUNK : (c + 1) * CHUNK, :].rearrange("(p j) w -> p j w", j=ROW_TILES)
+
         def load_rows(c):
             y_sb = y_pool.tile([P, ROW_TILES, WIDTH], BF16, name="y_sb")
-            nc.sync.dma_start(
-                out=y_sb[:],
-                in_=y_lanes[c * CHUNK : (c + 1) * CHUNK, :].rearrange("(p j) w -> p j w", j=ROW_TILES),
-            )
+            for j in range(ROW_TILES):
+                nc.sync.dma_start(out=y_sb[:, j, :], in_=chunk_rows(y_lanes, c)[:, j, :])
             y_tiles[c] = y_sb
-
-        load_rows(0)
 
         identity = consts.tile([P, P], F32, name="identity")
         make_identity(nc, identity[:])
+
+        bias_rows = consts.tile([P, P], BF16, name="bias_rows")
+        nc.vector.memset(bias_rows[:], 0.0)
+        n_bias = LANES * PACK
+        nc.sync.dma_start(out=bias_rows[0:n_bias, :], in_=b1.rearrange("g o (t p) -> (g o t) p", p=P))
+        nc.sync.dma_start(
+            out=bias_rows[n_bias : 2 * n_bias, :], in_=b2.rearrange("g o (t p) -> (g o t) p", p=P)
+        )
+        load_rows(0)
+        bias_rows_f32 = consts.tile([P, P], F32, name="bias_rows_f32")
+        nc.vector.tensor_copy(out=bias_rows_f32[:], in_=bias_rows[:])
+        bias_ps = ot_psum.tile([P, P], F32, name="bias_ps", tag="ot")
+        nc.tensor.transpose(bias_ps[:], bias_rows_f32[:], identity[:])
+        bias_col = consts.tile([P, 2 * n_bias], F32, name="bias_col")
+        nc.vector.tensor_copy(out=bias_col[:], in_=bias_ps[:, 0 : 2 * n_bias])
 
         w1_codes = consts.tile([P, LANES, FEAT], U32, name="w1_codes", align_bytes=64)
         w1_scales = consts.tile([P, LANES, FEAT], U8, name="w1_scales", align_bytes=64)
@@ -81,38 +97,19 @@ def tile_blockresmlp_mixerblock_pa_t_kernel(tc, y_lanes, w1, b1, w2, b2, out):
         load_rows(1)
         quantise_weights(nc, stage, w2, w2_codes, w2_scales)
 
-        b1_rows = consts.tile([P, P], BF16, name="b1_rows")
-        nc.vector.memset(b1_rows[:], 0.0)
-        nc.scalar.dma_start(
-            out=b1_rows[0 : LANES * PACK, :], in_=b1.rearrange("g o (t p) -> (g o t) p", p=P)
-        )
-        b1_rows_f32 = consts.tile([P, P], F32, name="b1_rows_f32")
-        nc.vector.tensor_copy(out=b1_rows_f32[:], in_=b1_rows[:])
-        b1_ps = zt_psum.tile([P, P], F32, name="b1_ps", tag="zt")
-        nc.tensor.transpose(b1_ps[:], b1_rows_f32[:], identity[:])
-        b1_col = consts.tile([P, LANES * PACK], F32, name="b1_col")
-        nc.vector.tensor_copy(out=b1_col[:], in_=b1_ps[:, 0 : LANES * PACK])
-
-        b2_rows = consts.tile([P, LANES, FEAT], BF16, name="b2_rows")
-        nc.scalar.dma_start(
-            out=b2_rows.rearrange("p g d -> p (g d)"),
-            in_=b2.rearrange("g o d -> (g o d)").partition_broadcast(P),
-        )
-        b2_all = consts.tile([P, FEAT, LANES], F32, name="b2_all")
-        nc.vector.tensor_copy(out=b2_all[:], in_=b2_rows.rearrange("p g d -> p d g"))
-
         def quantise_rows(c):
             y_sb = y_tiles[c]
             zg = z_pool.tile([P, LANES, CHUNK, PACK], BF16, name="zg", align_bytes=64)
             for j in range(ROW_TILES):
                 words = y_sb[:, j, :].bitcast(F32)
-                zt = zt_psum.tile([P, PACK, P], F32, name="zt", tag="zt")
+                zt = zt_psum.tile([P, PACK, P], F32, name="zt")
                 for t in range(PACK):
                     nc.tensor.transpose(zt[:, t, :], words[:, t * P : (t + 1) * P], identity[:])
-                nc.scalar.copy(
-                    out=zg[:, :, j * P : (j + 1) * P, :],
-                    in_=zt[:].bitcast(BF16).rearrange("p t (b g) -> p g b t", g=LANES),
-                )
+                split = zt[:].bitcast(BF16).rearrange("p t (b g) -> p g b t", g=LANES)
+                if j % 2 == 0:
+                    nc.scalar.copy(out=zg[:, :, j * P : (j + 1) * P, :], in_=split)
+                else:
+                    nc.vector.tensor_copy(out=zg[:, :, j * P : (j + 1) * P, :], in_=split)
             zc = z_pool.tile([P, LANES, CHUNK], U32, name="zc", align_bytes=64)
             zs = z_pool.tile([P, LANES, CHUNK], U8, name="zs", align_bytes=64)
             nc.vector.quantize_mx(
@@ -121,18 +118,6 @@ def tile_blockresmlp_mixerblock_pa_t_kernel(tc, y_lanes, w1, b1, w2, b2, out):
                 in_=zg.rearrange("p g b t -> p (g b t)"),
             )
             z_codes[c] = (zc, zs)
-
-        def add_bias_to_rows(c):
-            y_sb = y_tiles[c]
-            res = res_pool.tile([P, ROW_TILES, WIDTH], F32, name="res")
-            for j in range(ROW_TILES):
-                nc.vector.tensor_tensor(
-                    out=res[:, j, :],
-                    in0=y_sb[:, j, :],
-                    in1=b2_all.rearrange("p d g -> p (d g)"),
-                    op=ALU.add,
-                )
-            res_tiles[c] = res
 
         def hidden_layer(c):
             zc, zs = z_codes[c]
@@ -152,7 +137,7 @@ def tile_blockresmlp_mixerblock_pa_t_kernel(tc, y_lanes, w1, b1, w2, b2, out):
                         start=True,
                         stop=True,
                     )
-                    bias = b1_col[:, g * PACK + t : g * PACK + t + 1]
+                    bias = bias_col[:, g * PACK + t : g * PACK + t + 1]
                     nc.scalar.activation(out=exp_v[:, t, :], in_=acc[:], func=ACT.Exp, bias=bias, scale=1.0)
                     nc.scalar.activation(out=relu_v[:, t, :], in_=acc[:], func=ACT.Relu, bias=bias, scale=1.0)
                 hg = h_pool.tile([P, CHUNK, PACK], BF16, name="hg", align_bytes=64)
@@ -173,30 +158,47 @@ def tile_blockresmlp_mixerblock_pa_t_kernel(tc, y_lanes, w1, b1, w2, b2, out):
 
         def output_layer(c):
             hc, hs = h_codes[c]
-            res = res_tiles[c]
-            for j in range(ROW_TILES):
-                for half in range(FEAT // HALF):
-                    prod = l2_psum.tile([P, LANES, HALF], F32, name="prod")
-                    for g in range(LANES):
+            y_sb = y_tiles[c]
+            res = res_pool.tile([P, ROW_TILES, WIDTH], F32, name="res")
+            for half in range(HALVES):
+                prod_t = rt_pool.tile([P, LANES, BLOCKS, CHUNK], F32, name="prod_t")
+                for g in range(LANES):
+                    for m in range(BLOCKS):
+                        block = half * BLOCKS + m
+                        acc_t = l2_psum.tile([P, CHUNK], F32, name="acc_t")
                         nc.tensor.matmul_mx(
-                            out=prod[:, g, :],
-                            lhsT=hc[:, g, j * P : (j + 1) * P].bitcast(FP8X4),
-                            lhsT_scale=hs[:, g, j * P : (j + 1) * P],
-                            rhs=w2_codes[:, g, half * HALF : (half + 1) * HALF].bitcast(FP8X4),
-                            rhs_scale=w2_scales[:, g, half * HALF : (half + 1) * HALF],
+                            out=acc_t[:],
+                            lhsT=w2_codes[:, g, block * P : (block + 1) * P].bitcast(FP8X4),
+                            lhsT_scale=w2_scales[:, g, block * P : (block + 1) * P],
+                            rhs=hc[:, g, :].bitcast(FP8X4),
+                            rhs_scale=hs[:, g, :],
                             start=True,
                             stop=True,
                         )
-                    cols = res[:, j, half * LANES * HALF : (half + 1) * LANES * HALF].rearrange(
-                        "p (d g) -> p d g", g=LANES
-                    )
+                        col = n_bias + g * PACK + block
+                        nc.scalar.activation(
+                            out=prod_t[:, g, m, :],
+                            in_=acc_t[:],
+                            func=ACT.Identity,
+                            bias=bias_col[:, col : col + 1],
+                            scale=1.0,
+                        )
+                cols = slice(half * LANES * BLOCKS * P, (half + 1) * LANES * BLOCKS * P)
+                for j in range(ROW_TILES):
+                    ot = ot_psum.tile([P, LANES, BLOCKS, P], F32, name="ot")
+                    for g in range(LANES):
+                        for m in range(BLOCKS):
+                            nc.tensor.transpose(
+                                ot[:, g, m, :], prod_t[:, g, m, j * P : (j + 1) * P], identity[:]
+                            )
                     nc.vector.tensor_tensor(
-                        out=cols, in0=prod.rearrange("p g d -> p d g"), in1=cols, op=ALU.add
+                        out=res[:, j, cols].rearrange("p (d g) -> p d g", g=LANES),
+                        in0=ot.rearrange("p g m d -> p (m d) g"),
+                        in1=y_sb[:, j, cols].rearrange("p (d g) -> p d g", g=LANES),
+                        op=ALU.add,
                     )
-            nc.sync.dma_start(
-                out=out[c * CHUNK : (c + 1) * CHUNK, :].rearrange("(p j) w -> p j w", j=ROW_TILES),
-                in_=res[:],
-            )
+                    if half == HALVES - 1:
+                        nc.sync.dma_start(out=chunk_rows(out, c)[:, j, :], in_=res[:, j, :])
 
         for step in range(N_CHUNKS + 2):
             if step + 2 < N_CHUNKS:
@@ -205,6 +207,5 @@ def tile_blockresmlp_mixerblock_pa_t_kernel(tc, y_lanes, w1, b1, w2, b2, out):
                 quantise_rows(step)
             if 0 <= step - 1 < N_CHUNKS:
                 hidden_layer(step - 1)
-                add_bias_to_rows(step - 1)
             if 0 <= step - 2 < N_CHUNKS:
                 output_layer(step - 2)

@@ -18,28 +18,53 @@ ROWS = 4096
 FEAT = P * PACK
 WIDTH = LANES * FEAT
 CHUNK = 512
-ROW_TILES = CHUNK // P
-N_CHUNKS = ROWS // CHUNK
+CHUNKS = [CHUNK] * (ROWS // CHUNK)
 HALVES = 2
 BLOCKS = PACK // HALVES
+HALF_COLS = WIDTH // HALVES
 
 FLOPS = 2 * 2 * LANES * ROWS * FEAT * FEAT
 
 
-def quantise_weights(nc, stage, w, codes, scales):
-    raw = stage.tile([P, LANES, PACK, FEAT], BF16, name="raw")
-    nc.sync.dma_start(out=raw[:], in_=w.rearrange("g (t p) n -> p g t n", p=P))
-    for g in range(LANES):
-        grouped = stage.tile([P, FEAT, PACK], BF16, name="grouped", align_bytes=64)
-        nc.vector.tensor_copy(
-            out=grouped.rearrange("p (c i) t -> p c t i", i=4),
-            in_=raw[:, g].rearrange("p t (c i) -> p c t i", i=4),
-        )
-        nc.vector.quantize_mx(
-            out=codes[:, g, :].bitcast(FP8X4),
-            scales=scales[:, g, :],
-            in_=grouped.rearrange("p n t -> p (n t)"),
-        )
+def weave_lists(a, b):
+    woven = []
+    i = j = 0
+    while i < len(a) or j < len(b):
+        if j == len(b) or (i < len(a) and i * len(b) <= j * len(a)):
+            woven.append(a[i])
+            i += 1
+        else:
+            woven.append(b[j])
+            j += 1
+    return woven
+
+
+def weave(a, b):
+    for call in weave_lists(a, b):
+        call()
+
+
+def load_weights(nc, stage, w, g):
+    raw = stage.tile([P, PACK, FEAT], BF16, name="raw", bufs=2 * LANES)
+    nc.sync.dma_start(out=raw[:], in_=w[g].rearrange("(t p) n -> p t n", p=P))
+    return raw
+
+
+def group_weights(nc, stage, raw):
+    grouped = stage.tile([P, FEAT, PACK], BF16, name="grouped", align_bytes=64)
+    nc.vector.tensor_copy(
+        out=grouped.rearrange("p (c i) t -> p c t i", i=4),
+        in_=raw.rearrange("p t (c i) -> p c t i", i=4),
+    )
+    return grouped
+
+
+def quantise_weights(nc, grouped, codes, scales):
+    nc.vector.quantize_mx(
+        out=codes.bitcast(FP8X4),
+        scales=scales,
+        in_=grouped.rearrange("p n t -> p (n t)"),
+    )
 
 
 def tile_blockresmlp_mixerblock_pa_t_kernel(tc, y_lanes, w1, b1, w2, b2, out):
@@ -51,7 +76,8 @@ def tile_blockresmlp_mixerblock_pa_t_kernel(tc, y_lanes, w1, b1, w2, b2, out):
         z_pool = ctx.enter_context(tc.tile_pool(name="z_pool", bufs=2))
         elu_pool = ctx.enter_context(tc.tile_pool(name="elu_pool", bufs=2))
         h_pool = ctx.enter_context(tc.tile_pool(name="h_pool", bufs=2))
-        rt_pool = ctx.enter_context(tc.tile_pool(name="rt_pool", bufs=3))
+        rt_pool = ctx.enter_context(tc.tile_pool(name="rt_pool", bufs=2))
+        yb_pool = ctx.enter_context(tc.tile_pool(name="yb_pool", bufs=2))
         res_pool = ctx.enter_context(tc.tile_pool(name="res_pool", bufs=2))
         zt_psum = ctx.enter_context(tc.psum_pool(name="zt_psum", bufs=2))
         l1_psum = ctx.enter_context(tc.psum_pool(name="l1_psum", bufs=2))
@@ -62,150 +88,267 @@ def tile_blockresmlp_mixerblock_pa_t_kernel(tc, y_lanes, w1, b1, w2, b2, out):
         z_codes = {}
         h_codes = {}
 
+        def row_tiles(c):
+            return CHUNKS[c] // P
+
         def chunk_rows(dram, c):
-            return dram[c * CHUNK : (c + 1) * CHUNK, :].rearrange("(p j) w -> p j w", j=ROW_TILES)
+            first = sum(CHUNKS[:c])
+            return dram[first : first + CHUNKS[c], :].rearrange("(p j) w -> p j w", j=row_tiles(c))
 
         def load_rows(c):
-            y_sb = y_pool.tile([P, ROW_TILES, WIDTH], BF16, name="y_sb")
-            for j in range(ROW_TILES):
+            y_sb = y_pool.tile([P, row_tiles(c), WIDTH], BF16, name="y_sb")
+            for j in range(row_tiles(c)):
                 nc.sync.dma_start(out=y_sb[:, j, :], in_=chunk_rows(y_lanes, c)[:, j, :])
             y_tiles[c] = y_sb
 
-        identity = consts.tile([P, P], F32, name="identity")
-        make_identity(nc, identity[:])
-
         bias_rows = consts.tile([P, P], BF16, name="bias_rows")
-        nc.vector.memset(bias_rows[:], 0.0)
+        nc.gpsimd.memset(bias_rows[:], 0.0)
         n_bias = LANES * PACK
-        nc.sync.dma_start(out=bias_rows[0:n_bias, :], in_=b1.rearrange("g o (t p) -> (g o t) p", p=P))
-        nc.sync.dma_start(
+        nc.scalar.dma_start(out=bias_rows[0:n_bias, :], in_=b1.rearrange("g o (t p) -> (g o t) p", p=P))
+        nc.scalar.dma_start(
             out=bias_rows[n_bias : 2 * n_bias, :], in_=b2.rearrange("g o (t p) -> (g o t) p", p=P)
         )
-        load_rows(0)
-        bias_rows_f32 = consts.tile([P, P], F32, name="bias_rows_f32")
-        nc.vector.tensor_copy(out=bias_rows_f32[:], in_=bias_rows[:])
-        bias_ps = ot_psum.tile([P, P], F32, name="bias_ps", tag="ot")
-        nc.tensor.transpose(bias_ps[:], bias_rows_f32[:], identity[:])
+        identity = consts.tile([P, P], F32, name="identity")
+        make_identity(nc, identity[:])
         bias_col = consts.tile([P, 2 * n_bias], F32, name="bias_col")
-        nc.vector.tensor_copy(out=bias_col[:], in_=bias_ps[:, 0 : 2 * n_bias])
+
+        def turn_biases():
+            bias_rows_f32 = consts.tile([P, P], F32, name="bias_rows_f32")
+            nc.vector.tensor_copy(out=bias_rows_f32[:], in_=bias_rows[:])
+            bias_ps = ot_psum.tile([P, P], F32, name="bias_ps", tag="ot")
+            nc.tensor.transpose(bias_ps[:], bias_rows_f32[:], identity[:])
+            nc.vector.tensor_copy(out=bias_col[:], in_=bias_ps[:, 0 : 2 * n_bias])
 
         w1_codes = consts.tile([P, LANES, FEAT], U32, name="w1_codes", align_bytes=64)
         w1_scales = consts.tile([P, LANES, FEAT], U8, name="w1_scales", align_bytes=64)
         w2_codes = consts.tile([P, LANES, FEAT], U32, name="w2_codes", align_bytes=64)
         w2_scales = consts.tile([P, LANES, FEAT], U8, name="w2_scales", align_bytes=64)
-        quantise_weights(nc, stage, w1, w1_codes, w1_scales)
-        load_rows(1)
-        quantise_weights(nc, stage, w2, w2_codes, w2_scales)
+
+        b2_row = consts.tile([P, WIDTH], BF16, name="b2_row")
+
+        def spread_b2():
+            b2_lanes = stage.tile([P, LANES, FEAT], BF16, name="b2_lanes", bufs=1)
+            nc.sync.dma_start(out=b2_lanes[:], in_=b2.rearrange("g o d -> (g o) d").partition_broadcast(P))
+            nc.vector.tensor_copy(
+                out=b2_row.rearrange("p (d g) -> p d g", g=LANES), in_=b2_lanes.rearrange("p g d -> p d g")
+            )
+
+        zg_tiles = {}
+        elu_tiles = {}
+        hg_tiles = {}
+        prods = {}
+        ybs = {}
+        results = {}
+
+        def turn_rows(c, j, engine_copy):
+            if j == 0:
+                zg_tiles[c] = z_pool.tile([P, LANES, CHUNKS[c], PACK], BF16, name="zg", align_bytes=64)
+            words = y_tiles[c][:, j, :].bitcast(F32)
+            zt = zt_psum.tile([P, PACK, P], F32, name="zt")
+            for t in range(PACK):
+                nc.tensor.transpose(zt[:, t, :], words[:, t * P : (t + 1) * P], identity[:])
+            engine_copy(
+                out=zg_tiles[c][:, :, j * P : (j + 1) * P, :],
+                in_=zt[:].bitcast(BF16).rearrange("p t (b g) -> p g b t", g=LANES),
+            )
 
         def quantise_rows(c):
-            y_sb = y_tiles[c]
-            zg = z_pool.tile([P, LANES, CHUNK, PACK], BF16, name="zg", align_bytes=64)
-            for j in range(ROW_TILES):
-                words = y_sb[:, j, :].bitcast(F32)
-                zt = zt_psum.tile([P, PACK, P], F32, name="zt")
-                for t in range(PACK):
-                    nc.tensor.transpose(zt[:, t, :], words[:, t * P : (t + 1) * P], identity[:])
-                split = zt[:].bitcast(BF16).rearrange("p t (b g) -> p g b t", g=LANES)
-                if j % 2 == 0:
-                    nc.scalar.copy(out=zg[:, :, j * P : (j + 1) * P, :], in_=split)
-                else:
-                    nc.vector.tensor_copy(out=zg[:, :, j * P : (j + 1) * P, :], in_=split)
-            zc = z_pool.tile([P, LANES, CHUNK], U32, name="zc", align_bytes=64)
-            zs = z_pool.tile([P, LANES, CHUNK], U8, name="zs", align_bytes=64)
+            n = CHUNKS[c]
+            zc = z_pool.tile([P, LANES, n], U32, name="zc", align_bytes=64)
+            zs = z_pool.tile([P, LANES, n], U8, name="zs", align_bytes=64)
             nc.vector.quantize_mx(
                 out=zc.rearrange("p g b -> p (g b)").bitcast(FP8X4),
                 scales=zs.rearrange("p g b -> p (g b)"),
-                in_=zg.rearrange("p g b t -> p (g b t)"),
+                in_=zg_tiles[c].rearrange("p g b t -> p (g b t)"),
             )
             z_codes[c] = (zc, zs)
 
-        def hidden_layer(c):
+        def hidden_block(c, g, t):
+            n = CHUNKS[c]
+            if t == 0:
+                elu_tiles[c, g] = (
+                    elu_pool.tile([P, PACK, n], F32, name="exp_v"),
+                    elu_pool.tile([P, PACK, n], F32, name="relu_v"),
+                )
+            exp_v, relu_v = elu_tiles[c, g]
             zc, zs = z_codes[c]
-            hc = h_pool.tile([P, LANES, CHUNK], U32, name="hc", align_bytes=64)
-            hs = h_pool.tile([P, LANES, CHUNK], U8, name="hs", align_bytes=64)
-            for g in range(LANES):
-                exp_v = elu_pool.tile([P, PACK, CHUNK], F32, name="exp_v")
-                relu_v = elu_pool.tile([P, PACK, CHUNK], F32, name="relu_v")
-                for t in range(PACK):
-                    acc = l1_psum.tile([P, CHUNK], F32, name="acc")
-                    nc.tensor.matmul_mx(
-                        out=acc[:],
-                        lhsT=w1_codes[:, g, t * P : (t + 1) * P].bitcast(FP8X4),
-                        lhsT_scale=w1_scales[:, g, t * P : (t + 1) * P],
-                        rhs=zc[:, g, :].bitcast(FP8X4),
-                        rhs_scale=zs[:, g, :],
-                        start=True,
-                        stop=True,
-                    )
-                    bias = bias_col[:, g * PACK + t : g * PACK + t + 1]
-                    nc.scalar.activation(out=exp_v[:, t, :], in_=acc[:], func=ACT.Exp, bias=bias, scale=1.0)
-                    nc.scalar.activation(out=relu_v[:, t, :], in_=acc[:], func=ACT.Relu, bias=bias, scale=1.0)
-                hg = h_pool.tile([P, CHUNK, PACK], BF16, name="hg", align_bytes=64)
-                nc.vector.scalar_tensor_tensor(
-                    out=hg[:],
-                    in0=exp_v.rearrange("p t b -> p b t"),
-                    scalar=-1.0,
-                    in1=relu_v.rearrange("p t b -> p b t"),
-                    op0=ALU.add,
-                    op1=ALU.min,
-                )
-                nc.vector.quantize_mx(
-                    out=hc[:, g, :].bitcast(FP8X4),
-                    scales=hs[:, g, :],
-                    in_=hg.rearrange("p b t -> p (b t)"),
-                )
-            h_codes[c] = (hc, hs)
+            acc = l1_psum.tile([P, n], F32, name="acc")
+            nc.tensor.matmul_mx(
+                out=acc[:],
+                lhsT=w1_codes[:, g, t * P : (t + 1) * P].bitcast(FP8X4),
+                lhsT_scale=w1_scales[:, g, t * P : (t + 1) * P],
+                rhs=zc[:, g, :].bitcast(FP8X4),
+                rhs_scale=zs[:, g, :],
+                start=True,
+                stop=True,
+            )
+            bias = bias_col[:, g * PACK + t : g * PACK + t + 1]
+            nc.scalar.activation(out=exp_v[:, t, :], in_=acc[:], func=ACT.Exp, bias=bias, scale=1.0)
+            nc.scalar.activation(out=relu_v[:, t, :], in_=acc[:], func=ACT.Relu, bias=bias, scale=1.0)
 
-        def output_layer(c):
+        def combine(c, g):
+            exp_v, relu_v = elu_tiles[c, g]
+            hg = h_pool.tile([P, CHUNKS[c], PACK], BF16, name="hg", align_bytes=64)
+            nc.vector.scalar_tensor_tensor(
+                out=hg[:],
+                in0=exp_v.rearrange("p t b -> p b t"),
+                scalar=-1.0,
+                in1=relu_v.rearrange("p t b -> p b t"),
+                op0=ALU.add,
+                op1=ALU.min,
+            )
+            hg_tiles[c, g] = hg
+
+        def quantise_hidden(c, g):
+            if g == 0:
+                n = CHUNKS[c]
+                hc = h_pool.tile([P, LANES, n], U32, name="hc", align_bytes=64)
+                hs = h_pool.tile([P, LANES, n], U8, name="hs", align_bytes=64)
+                h_codes[c] = (hc, hs)
             hc, hs = h_codes[c]
-            y_sb = y_tiles[c]
-            res = res_pool.tile([P, ROW_TILES, WIDTH], F32, name="res")
-            for half in range(HALVES):
-                prod_t = rt_pool.tile([P, LANES, BLOCKS, CHUNK], F32, name="prod_t")
-                for g in range(LANES):
-                    for m in range(BLOCKS):
-                        block = half * BLOCKS + m
-                        acc_t = l2_psum.tile([P, CHUNK], F32, name="acc_t")
-                        nc.tensor.matmul_mx(
-                            out=acc_t[:],
-                            lhsT=w2_codes[:, g, block * P : (block + 1) * P].bitcast(FP8X4),
-                            lhsT_scale=w2_scales[:, g, block * P : (block + 1) * P],
-                            rhs=hc[:, g, :].bitcast(FP8X4),
-                            rhs_scale=hs[:, g, :],
-                            start=True,
-                            stop=True,
-                        )
-                        col = n_bias + g * PACK + block
-                        nc.scalar.activation(
-                            out=prod_t[:, g, m, :],
-                            in_=acc_t[:],
-                            func=ACT.Identity,
-                            bias=bias_col[:, col : col + 1],
-                            scale=1.0,
-                        )
-                cols = slice(half * LANES * BLOCKS * P, (half + 1) * LANES * BLOCKS * P)
-                for j in range(ROW_TILES):
-                    ot = ot_psum.tile([P, LANES, BLOCKS, P], F32, name="ot")
-                    for g in range(LANES):
-                        for m in range(BLOCKS):
-                            nc.tensor.transpose(
-                                ot[:, g, m, :], prod_t[:, g, m, j * P : (j + 1) * P], identity[:]
-                            )
-                    nc.vector.tensor_tensor(
-                        out=res[:, j, cols].rearrange("p (d g) -> p d g", g=LANES),
-                        in0=ot.rearrange("p g m d -> p (m d) g"),
-                        in1=y_sb[:, j, cols].rearrange("p (d g) -> p d g", g=LANES),
-                        op=ALU.add,
-                    )
-                    if half == HALVES - 1:
-                        nc.sync.dma_start(out=chunk_rows(out, c)[:, j, :], in_=res[:, j, :])
+            nc.vector.quantize_mx(
+                out=hc[:, g, :].bitcast(FP8X4),
+                scales=hs[:, g, :],
+                in_=hg_tiles[c, g].rearrange("p b t -> p (b t)"),
+            )
 
-        for step in range(N_CHUNKS + 2):
-            if step + 2 < N_CHUNKS:
-                load_rows(step + 2)
-            if step < N_CHUNKS:
-                quantise_rows(step)
-            if 0 <= step - 1 < N_CHUNKS:
-                hidden_layer(step - 1)
-            if 0 <= step - 2 < N_CHUNKS:
-                output_layer(step - 2)
+        def half_cols(half):
+            return slice(half * HALF_COLS, (half + 1) * HALF_COLS)
+
+        def turned_product(c, g, m):
+            if (g, m) == (0, 0):
+                prods[c] = rt_pool.tile([P, LANES, BLOCKS, CHUNKS[c]], F32, name="prod_t")
+            hc, hs = h_codes[c]
+            acc_t = l2_psum.tile([P, CHUNKS[c]], F32, name="acc_t")
+            nc.tensor.matmul_mx(
+                out=acc_t[:],
+                lhsT=w2_codes[:, g, m * P : (m + 1) * P].bitcast(FP8X4),
+                lhsT_scale=w2_scales[:, g, m * P : (m + 1) * P],
+                rhs=hc[:, g, :].bitcast(FP8X4),
+                rhs_scale=hs[:, g, :],
+                start=True,
+                stop=True,
+            )
+            col = n_bias + g * PACK + m
+            nc.scalar.activation(
+                out=prods[c][:, g, m, :],
+                in_=acc_t[:],
+                func=ACT.Identity,
+                bias=bias_col[:, col : col + 1],
+                scale=1.0,
+            )
+
+        def result_tile(c):
+            if c not in results:
+                results[c] = res_pool.tile([P, row_tiles(c), WIDTH], F32, name="res")
+            return results[c]
+
+        def finish_turned(c, j):
+            cols = half_cols(0)
+            ot = ot_psum.tile([P, LANES, BLOCKS, P], F32, name="ot")
+            for g in range(LANES):
+                for m in range(BLOCKS):
+                    nc.tensor.transpose(ot[:, g, m, :], prods[c][:, g, m, j * P : (j + 1) * P], identity[:])
+            nc.vector.tensor_tensor(
+                out=result_tile(c)[:, j, cols].rearrange("p (d g) -> p d g", g=LANES),
+                in0=ot.rearrange("p g m d -> p (m d) g"),
+                in1=y_tiles[c][:, j, cols].rearrange("p (d g) -> p d g", g=LANES),
+                op=ALU.add,
+            )
+            nc.sync.dma_start(out=chunk_rows(out, c)[:, j, :], in_=result_tile(c)[:, j, :])
+
+        def residual(c):
+            ybs[c] = yb_pool.tile([P, row_tiles(c), HALF_COLS], F32, name="yb")
+            nc.vector.tensor_tensor(
+                out=ybs[c][:],
+                in0=y_tiles[c][:, :, half_cols(1)],
+                in1=b2_row[:, half_cols(1)].unsqueeze(1).to_broadcast([P, row_tiles(c), HALF_COLS]),
+                op=ALU.add,
+            )
+
+        def finish_direct(c, j):
+            hc, hs = h_codes[c]
+            rows = slice(j * P, (j + 1) * P)
+            feats = slice(BLOCKS * P, FEAT)
+            direct = ot_psum.tile([P, LANES, BLOCKS * P], F32, name="direct", tag="ot")
+            for g in range(LANES):
+                nc.tensor.matmul_mx(
+                    out=direct[:, g, :],
+                    lhsT=hc[:, g, rows].bitcast(FP8X4),
+                    lhsT_scale=hs[:, g, rows],
+                    rhs=w2_codes[:, g, feats].bitcast(FP8X4),
+                    rhs_scale=w2_scales[:, g, feats],
+                    start=True,
+                    stop=True,
+                )
+            nc.vector.tensor_tensor(
+                out=result_tile(c)[:, j, half_cols(1)].rearrange("p (d g) -> p d g", g=LANES),
+                in0=direct.rearrange("p g d -> p d g"),
+                in1=ybs[c][:, j, :].rearrange("p (d g) -> p d g", g=LANES),
+                op=ALU.add,
+            )
+
+        n_chunks = len(CHUNKS)
+
+        def calls(step_function, c, *argument_lists):
+            if not 0 <= c < n_chunks:
+                return []
+            return [lambda arguments=arguments: step_function(c, *arguments) for arguments in argument_lists]
+
+        def row_calls(c, half):
+            if not 0 <= c < n_chunks:
+                return []
+            middle = (row_tiles(c) + 1) // 2
+            tiles = range(middle) if half == 0 else range(middle, row_tiles(c))
+            return calls(turn_rows, c, *[(j, nc.scalar.copy) for j in tiles])
+
+        def prepare_w2():
+            for g in range(LANES):
+                grouped = group_weights(nc, stage, raw_w2[g])
+                quantise_weights(nc, grouped, w2_codes[:, g, :], w2_scales[:, g, :])
+
+        ctx.enter_context(tc.manual_schedule())
+        load_rows(0)
+        raw_w1 = [load_weights(nc, stage, w1, g) for g in range(LANES)]
+        load_rows(1)
+        raw_w2 = [load_weights(nc, stage, w2, g) for g in range(LANES)]
+        load_rows(2)
+        for j in range(row_tiles(0)):
+            turn_rows(0, j, nc.scalar.copy if j % 2 == 0 else nc.vector.tensor_copy)
+        turn_biases()
+        w1_grouped = group_weights(nc, stage, raw_w1[0])
+        quantise_rows(0)
+        quantise_weights(nc, w1_grouped, w1_codes[:, 0, :], w1_scales[:, 0, :])
+        w1_grouped = group_weights(nc, stage, raw_w1[1])
+        quantise_weights(nc, w1_grouped, w1_codes[:, 1, :], w1_scales[:, 1, :])
+        for call in row_calls(1, 0):
+            call()
+
+        for c in range(n_chunks + 2):
+            if 3 <= c + 3 < n_chunks:
+                load_rows(c + 3)
+            tiles = range(row_tiles(c - 2)) if c - 2 >= 0 else []
+            finishes = calls(finish_turned, c - 2, *[(j,) for j in tiles])
+            middle = len(finishes) // 2
+            weave(
+                weave_lists(calls(hidden_block, c, *[(0, t) for t in range(PACK)]), row_calls(c + 1, 1))
+                + calls(turned_product, c - 1, *[(0, m) for m in range(BLOCKS)]),
+                calls(combine, c - 1, (1,))
+                + finishes[:middle]
+                + calls(quantise_hidden, c - 1, (1,))
+                + finishes[middle:]
+                + ([prepare_w2, spread_b2] if c == 0 else [])
+                + calls(residual, c - 1, ()),
+            )
+            tiles = range(row_tiles(c - 1)) if 0 <= c - 1 < n_chunks else []
+            finishes = calls(finish_direct, c - 1, *[(j,) for j in tiles])
+            middle = len(finishes) // 2
+            weave(
+                weave_lists(calls(hidden_block, c, *[(1, t) for t in range(PACK)]), row_calls(c + 2, 0))
+                + calls(turned_product, c - 1, *[(1, m) for m in range(BLOCKS)]),
+                calls(combine, c, (0,))
+                + finishes[:middle]
+                + calls(quantise_hidden, c, (0,))
+                + finishes[middle:]
+                + calls(quantise_rows, c + 1, ()),
+            )

@@ -79,10 +79,7 @@ def tile_blockresmlp_mixerblock_pa_t_kernel(tc, y_lanes, w1, b1, w2, b2, out):
         rt_pool = ctx.enter_context(tc.tile_pool(name="rt_pool", bufs=2))
         yb_pool = ctx.enter_context(tc.tile_pool(name="yb_pool", bufs=2))
         res_pool = ctx.enter_context(tc.tile_pool(name="res_pool", bufs=2))
-        zt_psum = ctx.enter_context(tc.psum_pool(name="zt_psum", bufs=2))
-        l1_psum = ctx.enter_context(tc.psum_pool(name="l1_psum", bufs=2))
-        l2_psum = ctx.enter_context(tc.psum_pool(name="l2_psum", bufs=2))
-        ot_psum = ctx.enter_context(tc.psum_pool(name="ot_psum", bufs=2))
+        banks = ctx.enter_context(tc.psum_pool(name="banks", bufs=8))
 
         y_tiles = {}
         z_codes = {}
@@ -115,7 +112,7 @@ def tile_blockresmlp_mixerblock_pa_t_kernel(tc, y_lanes, w1, b1, w2, b2, out):
         def turn_biases():
             bias_rows_f32 = consts.tile([P, P], F32, name="bias_rows_f32")
             nc.vector.tensor_copy(out=bias_rows_f32[:], in_=bias_rows[:])
-            bias_ps = ot_psum.tile([P, P], F32, name="bias_ps", tag="ot")
+            bias_ps = banks.tile([P, P], F32, name="bias_ps", tag="bank")
             nc.tensor.transpose(bias_ps[:], bias_rows_f32[:], identity[:])
             nc.vector.tensor_copy(out=bias_col[:], in_=bias_ps[:, 0 : 2 * n_bias])
 
@@ -144,7 +141,7 @@ def tile_blockresmlp_mixerblock_pa_t_kernel(tc, y_lanes, w1, b1, w2, b2, out):
             if j == 0:
                 zg_tiles[c] = z_pool.tile([P, LANES, CHUNKS[c], PACK], BF16, name="zg", align_bytes=64)
             words = y_tiles[c][:, j, :].bitcast(F32)
-            zt = zt_psum.tile([P, PACK, P], F32, name="zt")
+            zt = banks.tile([P, PACK, P], F32, name="zt", tag="bank")
             for t in range(PACK):
                 nc.tensor.transpose(zt[:, t, :], words[:, t * P : (t + 1) * P], identity[:])
             engine_copy(
@@ -172,7 +169,7 @@ def tile_blockresmlp_mixerblock_pa_t_kernel(tc, y_lanes, w1, b1, w2, b2, out):
                 )
             exp_v, relu_v = elu_tiles[c, g]
             zc, zs = z_codes[c]
-            acc = l1_psum.tile([P, n], F32, name="acc")
+            acc = banks.tile([P, n], F32, name="acc", tag="bank")
             nc.tensor.matmul_mx(
                 out=acc[:],
                 lhsT=w1_codes[:, g, t * P : (t + 1) * P].bitcast(FP8X4),
@@ -219,7 +216,7 @@ def tile_blockresmlp_mixerblock_pa_t_kernel(tc, y_lanes, w1, b1, w2, b2, out):
             if (g, m) == (0, 0):
                 prods[c] = rt_pool.tile([P, LANES, BLOCKS, CHUNKS[c]], F32, name="prod_t")
             hc, hs = h_codes[c]
-            acc_t = l2_psum.tile([P, CHUNKS[c]], F32, name="acc_t")
+            acc_t = banks.tile([P, CHUNKS[c]], F32, name="acc_t", tag="bank")
             nc.tensor.matmul_mx(
                 out=acc_t[:],
                 lhsT=w2_codes[:, g, m * P : (m + 1) * P].bitcast(FP8X4),
@@ -245,7 +242,7 @@ def tile_blockresmlp_mixerblock_pa_t_kernel(tc, y_lanes, w1, b1, w2, b2, out):
 
         def finish_turned(c, j):
             cols = half_cols(0)
-            ot = ot_psum.tile([P, LANES, BLOCKS, P], F32, name="ot")
+            ot = banks.tile([P, LANES, BLOCKS, P], F32, name="ot", tag="bank")
             for g in range(LANES):
                 for m in range(BLOCKS):
                     nc.tensor.transpose(ot[:, g, m, :], prods[c][:, g, m, j * P : (j + 1) * P], identity[:])
@@ -270,7 +267,7 @@ def tile_blockresmlp_mixerblock_pa_t_kernel(tc, y_lanes, w1, b1, w2, b2, out):
             hc, hs = h_codes[c]
             rows = slice(j * P, (j + 1) * P)
             feats = slice(BLOCKS * P, FEAT)
-            direct = ot_psum.tile([P, LANES, BLOCKS * P], F32, name="direct", tag="ot")
+            direct = banks.tile([P, LANES, BLOCKS * P], F32, name="direct", tag="bank")
             for g in range(LANES):
                 nc.tensor.matmul_mx(
                     out=direct[:, g, :],

@@ -19,6 +19,7 @@ FEAT = P * PACK
 WIDTH = LANES * FEAT
 CHUNK = 512
 CHUNKS = [CHUNK] * (ROWS // CHUNK)
+TAIL_CHUNKS = 2
 HALVES = 2
 BLOCKS = PACK // HALVES
 HALF_COLS = WIDTH // HALVES
@@ -107,6 +108,8 @@ def tile_blockresmlp_mixerblock_pa_t_kernel(tc, y_lanes, w1, b1, w2, b2, out):
         )
         identity = consts.tile([P, P], F32, name="identity")
         make_identity(nc, identity[:])
+        identity_bf = consts.tile([P, P], BF16, name="identity_bf")
+        make_identity(nc, identity_bf[:])
         bias_col = consts.tile([P, 2 * n_bias], F32, name="bias_col")
 
         def turn_biases():
@@ -243,16 +246,36 @@ def tile_blockresmlp_mixerblock_pa_t_kernel(tc, y_lanes, w1, b1, w2, b2, out):
         def finish_turned(c, j):
             cols = half_cols(0)
             ot = banks.tile([P, LANES, BLOCKS, P], F32, name="ot", tag="bank")
+            by_scalar = c >= n_chunks - TAIL_CHUNKS
+            if by_scalar:
+                nc.tensor.matmul(
+                    out=ot.rearrange("p g m d -> p g (m d)"),
+                    lhsT=identity_bf[:],
+                    rhs=y_tiles[c][:, j, cols].rearrange("p (d g) -> p g d", g=LANES),
+                    start=True,
+                    stop=False,
+                )
             for g in range(LANES):
                 for m in range(BLOCKS):
-                    nc.tensor.transpose(ot[:, g, m, :], prods[c][:, g, m, j * P : (j + 1) * P], identity[:])
-            nc.vector.tensor_tensor(
-                out=result_tile(c)[:, j, cols].rearrange("p (d g) -> p d g", g=LANES),
-                in0=ot.rearrange("p g m d -> p (m d) g"),
-                in1=y_tiles[c][:, j, cols].rearrange("p (d g) -> p d g", g=LANES),
-                op=ALU.add,
-            )
-            nc.sync.dma_start(out=chunk_rows(out, c)[:, j, :], in_=result_tile(c)[:, j, :])
+                    nc.tensor.matmul(
+                        out=ot[:, g, m, :],
+                        lhsT=prods[c][:, g, m, j * P : (j + 1) * P],
+                        rhs=identity[:],
+                        is_transpose=True,
+                        start=not by_scalar,
+                        stop=not by_scalar or (g, m) == (LANES - 1, BLOCKS - 1),
+                    )
+            bank = ot.rearrange("p g m d -> p (m d) g")
+            res = result_tile(c)[:, j, cols].rearrange("p (d g) -> p d g", g=LANES)
+            if by_scalar:
+                nc.scalar.copy(out=res, in_=bank)
+            else:
+                y = y_tiles[c][:, j, cols].rearrange("p (d g) -> p d g", g=LANES)
+                nc.vector.tensor_tensor(out=res, in0=bank, in1=y, op=ALU.add)
+            if c == n_chunks - 1:
+                nc.sync.dma_start(out=chunk_rows(out, c)[:, j, cols], in_=result_tile(c)[:, j, cols])
+            else:
+                nc.sync.dma_start(out=chunk_rows(out, c)[:, j, :], in_=result_tile(c)[:, j, :])
 
         def residual(c):
             ybs[c] = yb_pool.tile([P, row_tiles(c), HALF_COLS], F32, name="yb")
@@ -284,6 +307,10 @@ def tile_blockresmlp_mixerblock_pa_t_kernel(tc, y_lanes, w1, b1, w2, b2, out):
                 in1=ybs[c][:, j, :].rearrange("p (d g) -> p d g", g=LANES),
                 op=ALU.add,
             )
+            if c == n_chunks - 1:
+                nc.sync.dma_start(
+                    out=chunk_rows(out, c)[:, j, half_cols(1)], in_=result_tile(c)[:, j, half_cols(1)]
+                )
 
         n_chunks = len(CHUNKS)
 
@@ -292,12 +319,15 @@ def tile_blockresmlp_mixerblock_pa_t_kernel(tc, y_lanes, w1, b1, w2, b2, out):
                 return []
             return [lambda arguments=arguments: step_function(c, *arguments) for arguments in argument_lists]
 
+        def split_copy(c, j):
+            return nc.vector.tensor_copy if c % 2 == 1 and j == row_tiles(c) - 1 else nc.scalar.copy
+
         def row_calls(c, half):
             if not 0 <= c < n_chunks:
                 return []
             middle = (row_tiles(c) + 1) // 2
             tiles = range(middle) if half == 0 else range(middle, row_tiles(c))
-            return calls(turn_rows, c, *[(j, nc.scalar.copy) for j in tiles])
+            return calls(turn_rows, c, *[(j, split_copy(c, j)) for j in tiles])
 
         def prepare_w2():
             for g in range(LANES):
@@ -327,13 +357,17 @@ def tile_blockresmlp_mixerblock_pa_t_kernel(tc, y_lanes, w1, b1, w2, b2, out):
             tiles = range(row_tiles(c - 2)) if c - 2 >= 0 else []
             finishes = calls(finish_turned, c - 2, *[(j,) for j in tiles])
             middle = len(finishes) // 2
+            by_scalar = c - 2 >= n_chunks - TAIL_CHUNKS
             weave(
-                weave_lists(calls(hidden_block, c, *[(0, t) for t in range(PACK)]), row_calls(c + 1, 1))
-                + calls(turned_product, c - 1, *[(0, m) for m in range(BLOCKS)]),
+                weave_lists(
+                    calls(hidden_block, c, *[(0, t) for t in range(PACK)]),
+                    calls(turned_product, c - 1, *[(0, m) for m in range(BLOCKS)]) + row_calls(c + 1, 1),
+                )
+                + (finishes if by_scalar else []),
                 calls(combine, c - 1, (1,))
-                + finishes[:middle]
+                + ([] if by_scalar else finishes[:middle])
                 + calls(quantise_hidden, c - 1, (1,))
-                + finishes[middle:]
+                + ([] if by_scalar else finishes[middle:])
                 + ([prepare_w2, spread_b2] if c == 0 else [])
                 + calls(residual, c - 1, ()),
             )
@@ -341,11 +375,14 @@ def tile_blockresmlp_mixerblock_pa_t_kernel(tc, y_lanes, w1, b1, w2, b2, out):
             finishes = calls(finish_direct, c - 1, *[(j,) for j in tiles])
             middle = len(finishes) // 2
             weave(
-                weave_lists(calls(hidden_block, c, *[(1, t) for t in range(PACK)]), row_calls(c + 2, 0))
-                + calls(turned_product, c - 1, *[(1, m) for m in range(BLOCKS)]),
+                weave_lists(
+                    calls(hidden_block, c, *[(1, t) for t in range(PACK)]),
+                    calls(turned_product, c - 1, *[(1, m) for m in range(BLOCKS)]) + row_calls(c + 2, 0),
+                ),
                 calls(combine, c, (0,))
-                + finishes[:middle]
+                + finishes[:1]
+                + calls(quantise_rows, c + 1, ())
+                + finishes[1:middle]
                 + calls(quantise_hidden, c, (0,))
-                + finishes[middle:]
-                + calls(quantise_rows, c + 1, ()),
+                + finishes[middle:],
             )

@@ -19,7 +19,7 @@ FEAT = P * PACK
 WIDTH = LANES * FEAT
 CHUNK = 512
 CHUNKS = [CHUNK] * (ROWS // CHUNK)
-TAIL_CHUNKS = 2
+TAIL_CHUNKS = 3
 HALVES = 2
 BLOCKS = PACK // HALVES
 HALF_COLS = WIDTH // HALVES
@@ -168,7 +168,7 @@ def tile_blockresmlp_mixerblock_pa_t_kernel(tc, y_lanes, w1, b1, w2, b2, out):
             if t == 0:
                 elu_tiles[c, g] = (
                     elu_pool.tile([P, PACK, n], F32, name="exp_v"),
-                    elu_pool.tile([P, PACK, n], F32, name="relu_v"),
+                    elu_pool.tile([P, PACK, n], BF16, name="relu_v"),
                 )
             exp_v, relu_v = elu_tiles[c, g]
             zc, zs = z_codes[c]
@@ -319,15 +319,12 @@ def tile_blockresmlp_mixerblock_pa_t_kernel(tc, y_lanes, w1, b1, w2, b2, out):
                 return []
             return [lambda arguments=arguments: step_function(c, *arguments) for arguments in argument_lists]
 
-        def split_copy(c, j):
-            return nc.vector.tensor_copy if c % 2 == 1 and j == row_tiles(c) - 1 else nc.scalar.copy
-
         def row_calls(c, half):
             if not 0 <= c < n_chunks:
                 return []
             middle = (row_tiles(c) + 1) // 2
             tiles = range(middle) if half == 0 else range(middle, row_tiles(c))
-            return calls(turn_rows, c, *[(j, split_copy(c, j)) for j in tiles])
+            return calls(turn_rows, c, *[(j, nc.scalar.copy) for j in tiles])
 
         def prepare_w2():
             for g in range(LANES):
@@ -374,11 +371,10 @@ def tile_blockresmlp_mixerblock_pa_t_kernel(tc, y_lanes, w1, b1, w2, b2, out):
             tiles = range(row_tiles(c - 1)) if 0 <= c - 1 < n_chunks else []
             finishes = calls(finish_direct, c - 1, *[(j,) for j in tiles])
             middle = len(finishes) // 2
+            hidden = calls(hidden_block, c, *[(1, t) for t in range(PACK)])
+            products = calls(turned_product, c - 1, *[(1, m) for m in range(BLOCKS)])
             weave(
-                weave_lists(
-                    calls(hidden_block, c, *[(1, t) for t in range(PACK)]),
-                    calls(turned_product, c - 1, *[(1, m) for m in range(BLOCKS)]) + row_calls(c + 2, 0),
-                ),
+                hidden + products if c == n_chunks - 1 else weave_lists(hidden, products + row_calls(c + 2, 0)),
                 calls(combine, c, (0,))
                 + finishes[:1]
                 + calls(quantise_rows, c + 1, ())

@@ -13,6 +13,7 @@ ACT = mybir.ActivationFunctionType
 
 P = 128
 PACK = 4
+PAIRS = PACK // 2
 LANES = 2
 ROWS = 4096
 FEAT = P * PACK
@@ -135,6 +136,7 @@ def tile_blockresmlp_mixerblock_pa_t_kernel(tc, y_lanes, w1, b1, w2, b2, out):
 
         zg_tiles = {}
         elu_tiles = {}
+        pair_tiles = {}
         hg_tiles = {}
         prods = {}
         ybs = {}
@@ -188,15 +190,21 @@ def tile_blockresmlp_mixerblock_pa_t_kernel(tc, y_lanes, w1, b1, w2, b2, out):
 
         def combine(c, g):
             exp_v, relu_v = elu_tiles[c, g]
-            hg = h_pool.tile([P, CHUNKS[c], PACK], BF16, name="hg", align_bytes=64)
-            nc.vector.scalar_tensor_tensor(
-                out=hg[:],
-                in0=exp_v.rearrange("p t b -> p b t"),
-                scalar=-1.0,
-                in1=relu_v.rearrange("p t b -> p b t"),
-                op0=ALU.add,
-                op1=ALU.min,
-            )
+            pairs = h_pool.tile([P, PAIRS, CHUNKS[c], 2], BF16, name="pairs")
+            for u in range(PAIRS):
+                nc.vector.scalar_tensor_tensor(
+                    out=pairs[:, u],
+                    in0=exp_v[:, 2 * u : 2 * u + 2, :].rearrange("p e b -> p b e"),
+                    scalar=-1.0,
+                    in1=relu_v[:, 2 * u : 2 * u + 2, :].rearrange("p e b -> p b e"),
+                    op0=ALU.add,
+                    op1=ALU.min,
+                )
+            pair_tiles[c, g] = pairs
+
+        def interleave(c, g):
+            hg = h_pool.tile([P, CHUNKS[c], PAIRS, 2], BF16, name="hg", align_bytes=64)
+            nc.vector.tensor_copy(out=hg[:], in_=pair_tiles[c, g].rearrange("p u b e -> p b u e"))
             hg_tiles[c, g] = hg
 
         def quantise_hidden(c, g):
@@ -209,7 +217,7 @@ def tile_blockresmlp_mixerblock_pa_t_kernel(tc, y_lanes, w1, b1, w2, b2, out):
             nc.vector.quantize_mx(
                 out=hc[:, g, :].bitcast(FP8X4),
                 scales=hs[:, g, :],
-                in_=hg_tiles[c, g].rearrange("p b t -> p (b t)"),
+                in_=hg_tiles[c, g].rearrange("p b u e -> p (b u e)"),
             )
 
         def half_cols(half):
@@ -319,12 +327,15 @@ def tile_blockresmlp_mixerblock_pa_t_kernel(tc, y_lanes, w1, b1, w2, b2, out):
                 return []
             return [lambda arguments=arguments: step_function(c, *arguments) for arguments in argument_lists]
 
+        def split_copy(c, j):
+            return nc.vector.tensor_copy if c % 2 == 1 and j == row_tiles(c) - 1 else nc.scalar.copy
+
         def row_calls(c, half):
             if not 0 <= c < n_chunks:
                 return []
             middle = (row_tiles(c) + 1) // 2
             tiles = range(middle) if half == 0 else range(middle, row_tiles(c))
-            return calls(turn_rows, c, *[(j, nc.scalar.copy) for j in tiles])
+            return calls(turn_rows, c, *[(j, split_copy(c, j)) for j in tiles])
 
         def prepare_w2():
             for g in range(LANES):
@@ -362,7 +373,9 @@ def tile_blockresmlp_mixerblock_pa_t_kernel(tc, y_lanes, w1, b1, w2, b2, out):
                 )
                 + (finishes if by_scalar else []),
                 calls(combine, c - 1, (1,))
-                + ([] if by_scalar else finishes[:middle])
+                + ([] if by_scalar else finishes[:1])
+                + calls(interleave, c - 1, (1,))
+                + ([] if by_scalar else finishes[1:middle])
                 + calls(quantise_hidden, c - 1, (1,))
                 + ([] if by_scalar else finishes[middle:])
                 + ([prepare_w2, spread_b2] if c == 0 else [])
@@ -377,6 +390,7 @@ def tile_blockresmlp_mixerblock_pa_t_kernel(tc, y_lanes, w1, b1, w2, b2, out):
                 hidden + products if c == n_chunks - 1 else weave_lists(hidden, products + row_calls(c + 2, 0)),
                 calls(combine, c, (0,))
                 + finishes[:1]
+                + calls(interleave, c, (0,))
                 + calls(quantise_rows, c + 1, ())
                 + finishes[1:middle]
                 + calls(quantise_hidden, c, (0,))

@@ -21,6 +21,7 @@ WIDTH = LANES * FEAT
 CHUNK = 512
 CHUNKS = [CHUNK] * (ROWS // CHUNK)
 TAIL_CHUNKS = 3
+VECTOR_SPLITS = (1, 3)
 HALVES = 2
 BLOCKS = PACK // HALVES
 HALF_COLS = WIDTH // HALVES
@@ -113,9 +114,9 @@ def tile_blockresmlp_mixerblock_pa_t_kernel(tc, y_lanes, w1, b1, w2, b2, out):
         make_identity(nc, identity_bf[:])
         bias_col = consts.tile([P, 2 * n_bias], F32, name="bias_col")
 
+        bias_rows_f32 = consts.tile([P, P], F32, name="bias_rows_f32")
+
         def turn_biases():
-            bias_rows_f32 = consts.tile([P, P], F32, name="bias_rows_f32")
-            nc.vector.tensor_copy(out=bias_rows_f32[:], in_=bias_rows[:])
             bias_ps = banks.tile([P, P], F32, name="bias_ps", tag="bank")
             nc.tensor.transpose(bias_ps[:], bias_rows_f32[:], identity[:])
             nc.vector.tensor_copy(out=bias_col[:], in_=bias_ps[:, 0 : 2 * n_bias])
@@ -127,9 +128,9 @@ def tile_blockresmlp_mixerblock_pa_t_kernel(tc, y_lanes, w1, b1, w2, b2, out):
 
         b2_row = consts.tile([P, WIDTH], BF16, name="b2_row")
 
+        b2_lanes = consts.tile([P, LANES, FEAT], BF16, name="b2_lanes")
+
         def spread_b2():
-            b2_lanes = stage.tile([P, LANES, FEAT], BF16, name="b2_lanes", bufs=1)
-            nc.sync.dma_start(out=b2_lanes[:], in_=b2.rearrange("g o d -> (g o) d").partition_broadcast(P))
             nc.vector.tensor_copy(
                 out=b2_row.rearrange("p (d g) -> p d g", g=LANES), in_=b2_lanes.rearrange("p g d -> p d g")
             )
@@ -328,7 +329,7 @@ def tile_blockresmlp_mixerblock_pa_t_kernel(tc, y_lanes, w1, b1, w2, b2, out):
             return [lambda arguments=arguments: step_function(c, *arguments) for arguments in argument_lists]
 
         def split_copy(c, j):
-            return nc.vector.tensor_copy if c % 2 == 1 and j == row_tiles(c) - 1 else nc.scalar.copy
+            return nc.vector.tensor_copy if c in VECTOR_SPLITS and j == row_tiles(c) - 1 else nc.scalar.copy
 
         def row_calls(c, half):
             if not 0 <= c < n_chunks:
@@ -344,12 +345,17 @@ def tile_blockresmlp_mixerblock_pa_t_kernel(tc, y_lanes, w1, b1, w2, b2, out):
 
         ctx.enter_context(tc.manual_schedule())
         load_rows(0)
-        raw_w1 = [load_weights(nc, stage, w1, g) for g in range(LANES)]
+        raw_w1 = [load_weights(nc, stage, w1, 0)]
         load_rows(1)
+        raw_w1.append(load_weights(nc, stage, w1, 1))
+        nc.sync.dma_start(out=b2_lanes[:], in_=b2.rearrange("g o d -> (g o) d").partition_broadcast(P))
         raw_w2 = [load_weights(nc, stage, w2, g) for g in range(LANES)]
         load_rows(2)
-        for j in range(row_tiles(0)):
-            turn_rows(0, j, nc.scalar.copy if j % 2 == 0 else nc.vector.tensor_copy)
+        turn_rows(0, 0, nc.scalar.copy)
+        nc.vector.tensor_copy(out=bias_rows_f32[:], in_=bias_rows[:])
+        turn_rows(0, 1, nc.vector.tensor_copy)
+        for j in range(2, row_tiles(0)):
+            turn_rows(0, j, nc.scalar.copy)
         turn_biases()
         w1_grouped = group_weights(nc, stage, raw_w1[0])
         quantise_rows(0)

from contextlib import ExitStack

import concourse.mybir as mybir
from concourse.masks import make_identity

F32 = mybir.dt.float32
BF16 = mybir.dt.bfloat16
U32 = mybir.dt.uint32
U8 = mybir.dt.uint8
FP8X4 = mybir.dt.float8_e4m3fn_x4
ALU = mybir.AluOpType
ACT = mybir.ActivationFunctionType

P = 128
PACK = 4
PAIRS = PACK // 2
LANES = 2
ROWS = 4096
FEAT = P * PACK
WIDTH = LANES * FEAT
CHUNK = 512
CHUNKS = [CHUNK] * (ROWS // CHUNK)
TAIL_CHUNKS = 3
VECTOR_SPLITS = (1, 3)
HALVES = 2
BLOCKS = PACK // HALVES
HALF_COLS = WIDTH // HALVES

FLOPS = 2 * 2 * LANES * ROWS * FEAT * FEAT


def weave_lists(a, b):
    woven = []
    i = j = 0
    while i < len(a) or j < len(b):
        if j == len(b) or (i < len(a) and i * len(b) <= j * len(a)):
            woven.append(a[i])
            i += 1
        else:
            woven.append(b[j])
            j += 1
    return woven


def weave(a, b):
    for call in weave_lists(a, b):
        call()


def load_weights(nc, stage, w, g):
    raw = stage.tile([P, PACK, FEAT], BF16, name="raw", bufs=2 * LANES)
    nc.sync.dma_start(out=raw[:], in_=w[g].rearrange("(t p) n -> p t n", p=P))
    return raw


def group_weights(nc, stage, raw):
    grouped = stage.tile([P, FEAT, PACK], BF16, name="grouped", align_bytes=64)
    nc.vector.tensor_copy(
        out=grouped.rearrange("p (c i) t -> p c t i", i=4),
        in_=raw.rearrange("p t (c i) -> p c t i", i=4),
    )
    return grouped


def quantise_weights(nc, grouped, codes, scales):
    nc.vector.quantize_mx(
        out=codes.bitcast(FP8X4),
        scales=scales,
        in_=grouped.rearrange("p n t -> p (n t)"),
    )


def tile_blockresmlp_mixerblock_pa_t_kernel(tc, y_lanes, w1, b1, w2, b2, out):
    nc = tc.nc
    with ExitStack() as ctx:
        consts = ctx.enter_context(tc.tile_pool(name="consts", bufs=1))
        stage = ctx.enter_context(tc.tile_pool(name="stage", bufs=2))
        y_pool = ctx.enter_context(tc.tile_pool(name="y_pool", bufs=6))
        z_pool = ctx.enter_context(tc.tile_pool(name="z_pool", bufs=2))
        elu_pool = ctx.enter_context(tc.tile_pool(name="elu_pool", bufs=2))
        h_pool = ctx.enter_context(tc.tile_pool(name="h_pool", bufs=2))
        rt_pool = ctx.enter_context(tc.tile_pool(name="rt_pool", bufs=2))
        yb_pool = ctx.enter_context(tc.tile_pool(name="yb_pool", bufs=2))
        res_pool = ctx.enter_context(tc.tile_pool(name="res_pool", bufs=2))
        banks = ctx.enter_context(tc.psum_pool(name="banks", bufs=8))

        y_tiles = {}
        z_codes = {}
        h_codes = {}

        def row_tiles(c):
            return CHUNKS[c] // P

        def chunk_rows(dram, c):
            first = sum(CHUNKS[:c])
            return dram[first : first + CHUNKS[c], :].rearrange("(p j) w -> p j w", j=row_tiles(c))

        def load_rows(c):
            y_sb = y_pool.tile([P, row_tiles(c), WIDTH], BF16, name="y_sb")
            for j in range(row_tiles(c)):
                nc.sync.dma_start(out=y_sb[:, j, :], in_=chunk_rows(y_lanes, c)[:, j, :])
            y_tiles[c] = y_sb

        bias_rows = consts.tile([P, P], BF16, name="bias_rows")
        nc.gpsimd.memset(bias_rows[:], 0.0)
        n_bias = LANES * PACK
        nc.scalar.dma_start(out=bias_rows[0:n_bias, :], in_=b1.rearrange("g o (t p) -> (g o t) p", p=P))
        nc.scalar.dma_start(
            out=bias_rows[n_bias : 2 * n_bias, :], in_=b2.rearrange("g o (t p) -> (g o t) p", p=P)
        )
        identity = consts.tile([P, P], F32, name="identity")
        make_identity(nc, identity[:])
        identity_bf = consts.tile([P, P], BF16, name="identity_bf")
        make_identity(nc, identity_bf[:])
        bias_col = consts.tile([P, 2 * n_bias], F32, name="bias_col")

        bias_rows_f32 = consts.tile([P, P], F32, name="bias_rows_f32")

        def turn_biases():
            bias_ps = banks.tile([P, P], F32, name="bias_ps", tag="bank")
            nc.tensor.transpose(bias_ps[:], bias_rows_f32[:], identity[:])
            nc.vector.tensor_copy(out=bias_col[:], in_=bias_ps[:, 0 : 2 * n_bias])

        w1_codes = consts.tile([P, LANES, FEAT], U32, name="w1_codes", align_bytes=64)
        w1_scales = consts.tile([P, LANES, FEAT], U8, name="w1_scales", align_bytes=64)
        w2_codes = consts.tile([P, LANES, FEAT], U32, name="w2_codes", align_bytes=64)
        w2_scales = consts.tile([P, LANES, FEAT], U8, name="w2_scales", align_bytes=64)

        b2_row = consts.tile([P, WIDTH], BF16, name="b2_row")

        b2_lanes = consts.tile([P, LANES, FEAT], BF16, name="b2_lanes")

        def spread_b2():
            nc.vector.tensor_copy(
                out=b2_row.rearrange("p (d g) -> p d g", g=LANES), in_=b2_lanes.rearrange("p g d -> p d g")
            )

        zg_tiles = {}
        elu_tiles = {}
        pair_tiles = {}
        hg_tiles = {}
        prods = {}
        ybs = {}
        results = {}

        def turn_rows(c, j, engine_copy):
            if j == 0:
                zg_tiles[c] = z_pool.tile([P, LANES, CHUNKS[c], PACK], BF16, name="zg", align_bytes=64)
            words = y_tiles[c][:, j, :].bitcast(F32)
            zt = banks.tile([P, PACK, P], F32, name="zt", tag="bank")
            for t in range(PACK):
                nc.tensor.transpose(zt[:, t, :], words[:, t * P : (t + 1) * P], identity[:])
            engine_copy(
                out=zg_tiles[c][:, :, j * P : (j + 1) * P, :],
                in_=zt[:].bitcast(BF16).rearrange("p t (b g) -> p g b t", g=LANES),
            )

        def quantise_rows(c):
            n = CHUNKS[c]
            zc = z_pool.tile([P, LANES, n], U32, name="zc", align_bytes=64)
            zs = z_pool.tile([P, LANES, n], U8, name="zs", align_bytes=64)
            nc.vector.quantize_mx(
                out=zc.rearrange("p g b -> p (g b)").bitcast(FP8X4),
                scales=zs.rearrange("p g b -> p (g b)"),
                in_=zg_tiles[c].rearrange("p g b t -> p (g b t)"),
            )
            z_codes[c] = (zc, zs)

        def hidden_block(c, g, t):
            n = CHUNKS[c]
            if t == 0:
                elu_tiles[c, g] = (
                    elu_pool.tile([P, PACK, n], F32, name="exp_v"),
                    elu_pool.tile([P, PACK, n], BF16, name="relu_v"),
                )
            exp_v, relu_v = elu_tiles[c, g]
            zc, zs = z_codes[c]
            acc = banks.tile([P, n], F32, name="acc", tag="bank")
            nc.tensor.matmul_mx(
                out=acc[:],
                lhsT=w1_codes[:, g, t * P : (t + 1) * P].bitcast(FP8X4),
                lhsT_scale=w1_scales[:, g, t * P : (t + 1) * P],
                rhs=zc[:, g, :].bitcast(FP8X4),
                rhs_scale=zs[:, g, :],
                start=True,
                stop=True,
            )
            bias = bias_col[:, g * PACK + t : g * PACK + t + 1]
            nc.scalar.activation(out=exp_v[:, t, :], in_=acc[:], func=ACT.Exp, bias=bias, scale=1.0)
            nc.scalar.activation(out=relu_v[:, t, :], in_=acc[:], func=ACT.Relu, bias=bias, scale=1.0)

        def combine(c, g):
            exp_v, relu_v = elu_tiles[c, g]
            pairs = h_pool.tile([P, PAIRS, CHUNKS[c], 2], BF16, name="pairs")
            for u in range(PAIRS):
                nc.vector.scalar_tensor_tensor(
                    out=pairs[:, u],
                    in0=exp_v[:, 2 * u : 2 * u + 2, :].rearrange("p e b -> p b e"),
                    scalar=-1.0,
                    in1=relu_v[:, 2 * u : 2 * u + 2, :].rearrange("p e b -> p b e"),
                    op0=ALU.add,
                    op1=ALU.min,
                )
            pair_tiles[c, g] = pairs

        def interleave(c, g):
            hg = h_pool.tile([P, CHUNKS[c], PAIRS, 2], BF16, name="hg", align_bytes=64)
            nc.vector.tensor_copy(out=hg[:], in_=pair_tiles[c, g].rearrange("p u b e -> p b u e"))
            hg_tiles[c, g] = hg

        def quantise_hidden(c, g):
            if g == 0:
                n = CHUNKS[c]
                hc = h_pool.tile([P, LANES, n], U32, name="hc", align_bytes=64)
                hs = h_pool.tile([P, LANES, n], U8, name="hs", align_bytes=64)
                h_codes[c] = (hc, hs)
            hc, hs = h_codes[c]
            nc.vector.quantize_mx(
                out=hc[:, g, :].bitcast(FP8X4),
                scales=hs[:, g, :],
                in_=hg_tiles[c, g].rearrange("p b u e -> p (b u e)"),
            )

        def half_cols(half):
            return slice(half * HALF_COLS, (half + 1) * HALF_COLS)

        def turned_product(c, g, m):
            if (g, m) == (0, 0):
                prods[c] = rt_pool.tile([P, LANES, BLOCKS, CHUNKS[c]], F32, name="prod_t")
            hc, hs = h_codes[c]
            acc_t = banks.tile([P, CHUNKS[c]], F32, name="acc_t", tag="bank")
            nc.tensor.matmul_mx(
                out=acc_t[:],
                lhsT=w2_codes[:, g, m * P : (m + 1) * P].bitcast(FP8X4),
                lhsT_scale=w2_scales[:, g, m * P : (m + 1) * P],
                rhs=hc[:, g, :].bitcast(FP8X4),
                rhs_scale=hs[:, g, :],
                start=True,
                stop=True,
            )
            col = n_bias + g * PACK + m
            nc.scalar.activation(
                out=prods[c][:, g, m, :],
                in_=acc_t[:],
                func=ACT.Identity,
                bias=bias_col[:, col : col + 1],
                scale=1.0,
            )

        def result_tile(c):
            if c not in results:
                results[c] = res_pool.tile([P, row_tiles(c), WIDTH], F32, name="res")
            return results[c]

        def finish_turned(c, j):
            cols = half_cols(0)
            ot = banks.tile([P, LANES, BLOCKS, P], F32, name="ot", tag="bank")
            by_scalar = c >= n_chunks - TAIL_CHUNKS
            if by_scalar:
                nc.tensor.matmul(
                    out=ot.rearrange("p g m d -> p g (m d)"),
                    lhsT=identity_bf[:],
                    rhs=y_tiles[c][:, j, cols].rearrange("p (d g) -> p g d", g=LANES),
                    start=True,
                    stop=False,
                )
            for g in range(LANES):
                for m in range(BLOCKS):
                    nc.tensor.matmul(
                        out=ot[:, g, m, :],
                        lhsT=prods[c][:, g, m, j * P : (j + 1) * P],
                        rhs=identity[:],
                        is_transpose=True,
                        start=not by_scalar,
                        stop=not by_scalar or (g, m) == (LANES - 1, BLOCKS - 1),
                    )
            bank = ot.rearrange("p g m d -> p (m d) g")
            res = result_tile(c)[:, j, cols].rearrange("p (d g) -> p d g", g=LANES)
            if by_scalar:
                nc.scalar.copy(out=res, in_=bank)
            else:
                y = y_tiles[c][:, j, cols].rearrange("p (d g) -> p d g", g=LANES)
                nc.vector.tensor_tensor(out=res, in0=bank, in1=y, op=ALU.add)
            if c == n_chunks - 1:
                nc.sync.dma_start(out=chunk_rows(out, c)[:, j, cols], in_=result_tile(c)[:, j, cols])
            else:
                nc.sync.dma_start(out=chunk_rows(out, c)[:, j, :], in_=result_tile(c)[:, j, :])

        def residual(c):
            ybs[c] = yb_pool.tile([P, row_tiles(c), HALF_COLS], F32, name="yb")
            nc.vector.tensor_tensor(
                out=ybs[c][:],
                in0=y_tiles[c][:, :, half_cols(1)],
                in1=b2_row[:, half_cols(1)].unsqueeze(1).to_broadcast([P, row_tiles(c), HALF_COLS]),
                op=ALU.add,
            )

        def finish_direct(c, j):
            hc, hs = h_codes[c]
            rows = slice(j * P, (j + 1) * P)
            feats = slice(BLOCKS * P, FEAT)
            direct = banks.tile([P, LANES, BLOCKS * P], F32, name="direct", tag="bank")
            for g in range(LANES):
                nc.tensor.matmul_mx(
                    out=direct[:, g, :],
                    lhsT=hc[:, g, rows].bitcast(FP8X4),
                    lhsT_scale=hs[:, g, rows],
                    rhs=w2_codes[:, g, feats].bitcast(FP8X4),
                    rhs_scale=w2_scales[:, g, feats],
                    start=True,
                    stop=True,
                )
            nc.vector.tensor_tensor(
                out=result_tile(c)[:, j, half_cols(1)].rearrange("p (d g) -> p d g", g=LANES),
                in0=direct.rearrange("p g d -> p d g"),
                in1=ybs[c][:, j, :].rearrange("p (d g) -> p d g", g=LANES),
                op=ALU.add,
            )
            if c == n_chunks - 1:
                nc.sync.dma_start(
                    out=chunk_rows(out, c)[:, j, half_cols(1)], in_=result_tile(c)[:, j, half_cols(1)]
                )

        n_chunks = len(CHUNKS)

        def calls(step_function, c, *argument_lists):
            if not 0 <= c < n_chunks:
                return []
            return [lambda arguments=arguments: step_function(c, *arguments) for arguments in argument_lists]

        def split_copy(c, j):
            return nc.vector.tensor_copy if c in VECTOR_SPLITS and j == row_tiles(c) - 1 else nc.scalar.copy

        def row_calls(c, half):
            if not 0 <= c < n_chunks:
                return []
            middle = (row_tiles(c) + 1) // 2
            tiles = range(middle) if half == 0 else range(middle, row_tiles(c))
            return calls(turn_rows, c, *[(j, split_copy(c, j)) for j in tiles])

        def prepare_w2():
            for g in range(LANES):
                grouped = group_weights(nc, stage, raw_w2[g])
                quantise_weights(nc, grouped, w2_codes[:, g, :], w2_scales[:, g, :])

        ctx.enter_context(tc.manual_schedule())
        load_rows(0)
        raw_w1 = [load_weights(nc, stage, w1, 0)]
        load_rows(1)
        raw_w1.append(load_weights(nc, stage, w1, 1))
        nc.sync.dma_start(out=b2_lanes[:], in_=b2.rearrange("g o d -> (g o) d").partition_broadcast(P))
        raw_w2 = [load_weights(nc, stage, w2, g) for g in range(LANES)]
        load_rows(2)
        turn_rows(0, 0, nc.scalar.copy)
        nc.vector.tensor_copy(out=bias_rows_f32[:], in_=bias_rows[:])
        turn_rows(0, 1, nc.vector.tensor_copy)
        for j in range(2, row_tiles(0)):
            turn_rows(0, j, nc.scalar.copy)
        turn_biases()
        w1_grouped = group_weights(nc, stage, raw_w1[0])
        quantise_rows(0)
        quantise_weights(nc, w1_grouped, w1_codes[:, 0, :], w1_scales[:, 0, :])
        w1_grouped = group_weights(nc, stage, raw_w1[1])
        quantise_weights(nc, w1_grouped, w1_codes[:, 1, :], w1_scales[:, 1, :])
        for call in row_calls(1, 0):
            call()

        for c in range(n_chunks + 2):
            if 3 <= c + 3 < n_chunks:
                load_rows(c + 3)
            tiles = range(row_tiles(c - 2)) if c - 2 >= 0 else []
            finishes = calls(finish_turned, c - 2, *[(j,) for j in tiles])
            middle = len(finishes) // 2
            by_scalar = c - 2 >= n_chunks - TAIL_CHUNKS
            weave(
                weave_lists(
                    calls(hidden_block, c, *[(0, t) for t in range(PACK)]),
                    calls(turned_product, c - 1, *[(0, m) for m in range(BLOCKS)]) + row_calls(c + 1, 1),
                )
                + (finishes if by_scalar else []),
                calls(combine, c - 1, (1,))
                + ([] if by_scalar else finishes[:1])
                + calls(interleave, c - 1, (1,))
                + ([] if by_scalar else finishes[1:middle])
                + calls(quantise_hidden, c - 1, (1,))
                + ([] if by_scalar else finishes[middle:])
                + ([prepare_w2, spread_b2] if c == 0 else [])
                + calls(residual, c - 1, ()),
            )
            tiles = range(row_tiles(c - 1)) if 0 <= c - 1 < n_chunks else []
            finishes = calls(finish_direct, c - 1, *[(j,) for j in tiles])
            middle = len(finishes) // 2
            hidden = calls(hidden_block, c, *[(1, t) for t in range(PACK)])
            products = calls(turned_product, c - 1, *[(1, m) for m in range(BLOCKS)])
            weave(
                hidden + products if c == n_chunks - 1 else weave_lists(hidden, products + row_calls(c + 2, 0)),
                calls(combine, c, (0,))
                + finishes[:1]
                + calls(interleave, c, (0,))
                + calls(quantise_rows, c + 1, ())
                + finishes[1:middle]
                + calls(quantise_hidden, c, (0,))
                + finishes[middle:],
            )
